import numpy as np
import ml_dtypes


def mxq(x, axis, fmt="e4m3"):
    dtype, down = {"e4m3": (ml_dtypes.float8_e4m3fn, 7), "e5m2": (ml_dtypes.float8_e5m2, 14)}[fmt]
    v = np.moveaxis(np.asarray(x, np.float32).astype(ml_dtypes.bfloat16).astype(np.float64), axis, -1)
    blocks = v.reshape(v.shape[:-1] + (-1, 32))
    amax = np.abs(blocks).max(-1, keepdims=True)
    byte = np.maximum(np.where(amax > 0, np.frexp(amax)[1] - 1 + 127, 0) - down, 1)
    scale = np.exp2(byte - 127.0)
    codes = (blocks / scale).astype(np.float32).astype(dtype).astype(np.float64)
    return np.moveaxis((codes * scale).reshape(v.shape), -1, axis)


WIDE = False


def mx_kscale(k):
    if not WIDE:
        return np.ones(k)
    levels = np.array([10, -10, 5, -5, 0])
    a = np.random.permutation(np.resize(levels, k // 512 * 4)).reshape(k // 512, 4)
    idx = np.arange(k)
    return np.exp2(a[idx // 512, idx % 128 // 32])


BF16 = ml_dtypes.bfloat16


def bf(x):
    return np.asarray(x, np.float32).astype(BF16)


def f64(x):
    return np.asarray(x).astype(np.float64)


E2M1 = np.array([0.0, 0.5, 1.0, 1.5, 2.0, 3.0, 4.0, 6.0, -0.0, -0.5, -1.0, -1.5, -2.0, -3.0, -4.0, -6.0])


def pack_weight(w, fmt):
    k, n = w.shape
    w = f64(bf(w)).reshape(k // 32, 32, n)
    amax = np.abs(w).max(1)
    if fmt == "e4m3":
        byte = np.frexp(amax)[1] - 1 + 127 - 7
    else:
        mant, ex = np.frexp(amax / 6.0)
        byte = np.where(mant > 0.5, ex, ex - 1) + 127
    byte = np.clip(np.where(amax > 0, byte, 1), 1, 254)
    scaled = (w * np.exp2(127.0 - byte)[:, None, :]).reshape(k, n).astype(np.float32)
    by_word = np.ascontiguousarray(scaled.reshape(k // 512, 128, 4, n).transpose(0, 1, 3, 2))
    if fmt == "e4m3":
        words = by_word.astype(ml_dtypes.float8_e4m3fn).view(np.uint8)
    else:
        c = by_word.astype(ml_dtypes.float4_e2m1fn).view(np.uint8) & 0xF
        words = c[..., 0::2] | (c[..., 1::2] << 4)
    return np.ascontiguousarray(words), np.ascontiguousarray(byte.astype(np.uint8).reshape(k // 512, 16, n))


def unpack_weight(words, scales, fmt):
    g, p, n, _ = words.shape
    if fmt == "e4m3":
        vals = np.ascontiguousarray(words).view(ml_dtypes.float8_e4m3fn).astype(np.float64)
    else:
        nib = np.empty((g, p, n, 4), np.uint8)
        nib[..., 0::2] = words & 0xF
        nib[..., 1::2] = words >> 4
        vals = E2M1[nib]
    vals = vals * np.repeat(np.exp2(scales.astype(np.float64) - 127.0), 8, axis=1)[..., None]
    return vals.transpose(0, 1, 3, 2).reshape(g * 512, n)


B, P, L, FI, FO = 512, 2, 3, 512, 256
C = (L + 1) * (L + 1)
D = L + 1


def setup_inputs():
    s = mx_kscale(FI)
    x = bf(np.random.standard_normal((B, P, C, FI)) * s)
    we = np.random.standard_normal((L + 1, FI, FO)) / np.sqrt(FI) / s[:, None]
    wo = np.random.standard_normal((L + 1, FI, FO)) / np.sqrt(FI) / s[:, None]
    b = bf(np.random.standard_normal(FO) * 0.5)
    we_words, we_scales = pack_weight(we.reshape(-1, FO), "e4m3")
    wo_words, wo_scales = pack_weight(wo.reshape(-1, FO), "e4m3")
    return {"x": x,
            "W_e_words": we_words, "W_e_scales": we_scales,
            "W_o_words": wo_words, "W_o_scales": wo_scales,
            "b": b}


def reference(x, W_e_words, W_e_scales, W_o_words, W_o_scales, b):
    xq = mxq(f64(x), 3, "e4m3")
    weq = unpack_weight(W_e_words, W_e_scales, "e4m3").reshape(D, FI, FO)
    woq = unpack_weight(W_o_words, W_o_scales, "e4m3").reshape(D, FI, FO)
    outs_e, outs_o = [], []
    for l in range(L + 1):
        seg = xq[:, :, l * l:(l + 1) * (l + 1), :]
        oe = seg[:, 0] @ weq[l]
        if l == 0:
            oe = oe + f64(b)
        oo = seg[:, 1] @ woq[l]
        outs_e.append(oe)
        outs_o.append(oo)
    return np.stack([np.concatenate(outs_e, axis=-2), np.concatenate(outs_o, axis=-2)], axis=-3)

@@ -1,0 +1,164 @@
+from contextlib import ExitStack
+
+import concourse.mybir as mybir
+from concourse.masks import make_identity
+
+F32 = mybir.dt.float32
+BF16 = mybir.dt.bfloat16
+I32 = mybir.dt.int32
+U32 = mybir.dt.uint32
+U8 = mybir.dt.uint8
+FP8X4 = mybir.dt.float8_e4m3fn_x4
+
+P = 128
+PACK = 4
+ITEMS, PARITIES, COMPONENTS, F_IN, F_OUT = 512, 2, 16, 512, 256
+DEGREES = 4
+DEGREE_OF = [l for l in range(DEGREES) for m in range(2 * l + 1)]
+WORDS = F_IN // 2
+
+BLOCKS = 8
+BANK_BLOCKS = 2
+BANKS = BLOCKS // BANK_BLOCKS
+CHUNKS = [
+    (n0, parity, c0)
+    for n0 in range(0, ITEMS, P)
+    for parity in range(PARITIES)
+    for c0 in range(0, COMPONENTS, BLOCKS)
+]
+LOADS_AHEAD = 8
+OUT_BUFS = 6
+
+FLOPS = 2 * ITEMS * PARITIES * COMPONENTS * F_IN * F_OUT
+
+
+def tile_dense_pa_t_e_kernel(tc, x, W_e_words, W_e_scales, W_o_words, W_o_scales, b, out):
+    nc = tc.nc
+    with ExitStack() as ctx:
+        ctx.enter_context(tc.manual_schedule())
+        consts = ctx.enter_context(tc.tile_pool(name="consts", bufs=1))
+        x_pool = ctx.enter_context(tc.tile_pool(name="x_pool", bufs=LOADS_AHEAD))
+        grouped_pool = ctx.enter_context(tc.tile_pool(name="grouped_pool", bufs=2))
+        mx_pool = ctx.enter_context(tc.tile_pool(name="mx_pool", bufs=3))
+        out_pool = ctx.enter_context(tc.tile_pool(name="out_pool", bufs=OUT_BUFS))
+        psum_t = ctx.enter_context(tc.psum_pool(name="psum_t", bufs=BANKS))
+        psum_o = ctx.enter_context(tc.psum_pool(name="psum_o", bufs=BANKS))
+
+        w_scales = consts.tile([P, PARITIES, DEGREES, F_OUT], U8, align_bytes=64)
+        nc.vector.memset(w_scales[:].rearrange("p a l n -> p (a l n)").bitcast(I32), 0)
+        w_words = consts.tile([P, PARITIES, DEGREES, F_OUT], U32, align_bytes=64)
+
+        ident = consts.tile([P, P], F32)
+        make_identity(nc, ident[:])
+
+        ones = consts.tile([P, P], BF16)
+        nc.vector.memset(ones[:], 1.0)
+        bias_rows = consts.tile([P, BANK_BLOCKS * F_OUT], BF16)
+        nc.vector.memset(bias_rows[:], 0.0)
+        nc.scalar.dma_start(out=bias_rows[0:1, 0:F_OUT], in_=b.unsqueeze(0))
+        bias_psum = psum_o.tile([P, BANK_BLOCKS * F_OUT], F32, name="acc", tag="acc")
+        nc.tensor.matmul(out=bias_psum[:], lhsT=ones[:], rhs=bias_rows[:], start=True, stop=True)
+        bias_pair = consts.tile([P, BANK_BLOCKS * F_OUT], F32)
+        nc.vector.tensor_copy(out=bias_pair[:], in_=bias_psum[:])
+
+        def load_weights(parity, words, scales):
+            by_row = scales.rearrange("l (q r) n -> r q l n", r=4)
+            for r in range(4):
+                nc.sync.dma_start(
+                    out=w_scales[r : P : 32, parity].bitcast(I32), in_=by_row[r].bitcast(I32)
+                )
+            nc.sync.dma_start(
+                out=w_words[:, parity].bitcast(I32),
+                in_=words.rearrange("l p n t -> p l (n t)").bitcast(I32),
+            )
+
+        x_tiles = {}
+        grouped_tiles = {}
+        mx_tiles = {}
+
+        def load(g):
+            n0, parity, c0 = CHUNKS[g]
+            x_sb = x_pool.tile([P, BLOCKS, F_IN], BF16, name="x_sb", tag="x_sb")
+            nc.sync.dma_start(out=x_sb[:], in_=x[n0 : n0 + P, parity, c0 : c0 + BLOCKS, :])
+            x_tiles[g] = x_sb
+
+        def transpose(g):
+            x_words = x_tiles[g][:].bitcast(F32)
+            grouped = grouped_pool.tile(
+                [P, BLOCKS * P * PACK], BF16, align_bytes=64, name="grouped", tag="grouped"
+            )
+            grouped_words = grouped[:].bitcast(F32).rearrange(
+                "p (i r u) -> p i r u", i=BLOCKS, u=2
+            )
+            for bank in range(BANKS):
+                first = bank * BANK_BLOCKS
+                xt = psum_t.tile([P, BANK_BLOCKS, 2, P], F32, name="xt", tag="xt")
+                for j in range(BANK_BLOCKS):
+                    for u in range(2):
+                        nc.tensor.transpose(
+                            xt[:, j, u, :], x_words[:, first + j, u:WORDS:2], ident[:]
+                        )
+                nc.vector.tensor_copy(
+                    out=grouped_words[:, first : first + BANK_BLOCKS],
+                    in_=xt[:].rearrange("p j u r -> p j r u"),
+                )
+            grouped_tiles[g] = grouped
+
+        def quantise(g):
+            codes = mx_pool.tile([P, BLOCKS * P], U32, align_bytes=64, name="codes", tag="codes")
+            planes = mx_pool.tile([P, BLOCKS * P], U8, align_bytes=64, name="planes", tag="planes")
+            half = BLOCKS * P // 2
+            for h in range(2):
+                cols = slice(h * half, (h + 1) * half)
+                nc.vector.quantize_mx(
+                    out=codes[:, cols].bitcast(FP8X4),
+                    scales=planes[:, cols],
+                    in_=grouped_tiles[g][:, h * half * PACK : (h + 1) * half * PACK],
+                )
+            mx_tiles[g] = (codes, planes)
+
+        def multiply_and_store(g):
+            n0, parity, c0 = CHUNKS[g]
+            codes, planes = mx_tiles[g]
+            out_sb = out_pool.tile([P, BLOCKS * F_OUT], F32, name="out_sb", tag="out_sb")
+            for bank in range(BANKS):
+                first = bank * BANK_BLOCKS
+                acc = psum_o.tile([P, BANK_BLOCKS * F_OUT], F32, name="acc", tag="acc")
+                for j in range(BANK_BLOCKS):
+                    items = slice((first + j) * P, (first + j + 1) * P)
+                    degree = DEGREE_OF[c0 + first + j]
+                    nc.tensor.matmul_mx(
+                        out=acc[:, j * F_OUT : (j + 1) * F_OUT],
+                        lhsT=codes[:, items].bitcast(FP8X4),
+                        lhsT_scale=planes[:, items],
+                        rhs=w_words[:, parity, degree, :].bitcast(FP8X4),
+                        rhs_scale=w_scales[:, parity, degree, :],
+                        start=True,
+                        stop=True,
+                    )
+                result = out_sb[:, first * F_OUT : (first + BANK_BLOCKS) * F_OUT]
+                if parity == 0 and c0 + first == 0:
+                    nc.vector.tensor_tensor(
+                        out=result, in0=acc[:], in1=bias_pair[:], op=mybir.AluOpType.add
+                    )
+                else:
+                    nc.scalar.copy(out=result, in_=acc[:])
+            nc.sync.dma_start(
+                out=out[n0 : n0 + P, parity, c0 : c0 + BLOCKS, :].rearrange("n c f -> n (c f)"),
+                in_=out_sb[:],
+            )
+
+        for g in range(LOADS_AHEAD):
+            load(g)
+            if g == 0:
+                load_weights(0, W_e_words, W_e_scales)
+            if g == 1:
+                load_weights(1, W_o_words, W_o_scales)
+        transpose(0)
+        for g in range(len(CHUNKS)):
+            if g + LOADS_AHEAD < len(CHUNKS):
+                load(g + LOADS_AHEAD)
+            quantise(g)
+            if g + 1 < len(CHUNKS):
+                transpose(g + 1)
+            multiply_and_store(g)

@@ -17,17 +17,14 @@ DEGREES = 4
 DEGREE_OF = [l for l in range(DEGREES) for m in range(2 * l + 1)]
 WORDS = F_IN // 2
 
+CHUNKS = [(n0, parity) for n0 in range(0, ITEMS, P) for parity in range(PARITIES)]
 BLOCKS = 8
 BANK_BLOCKS = 2
 BANKS = BLOCKS // BANK_BLOCKS
-CHUNKS = [
-    (n0, parity, c0)
-    for n0 in range(0, ITEMS, P)
-    for parity in range(PARITIES)
-    for c0 in range(0, COMPONENTS, BLOCKS)
-]
-LOADS_AHEAD = 8
-OUT_BUFS = 6
+CHUNK_ROUNDS = COMPONENTS // BLOCKS
+ROUNDS = len(CHUNKS) * CHUNK_ROUNDS
+LOADS_AHEAD = 4
+OUT_BUFS = 4
 
 FLOPS = 2 * ITEMS * PARITIES * COMPONENTS * F_IN * F_OUT
 
@@ -75,15 +72,17 @@ def tile_dense_pa_t_e_kernel(tc, x, W_e_words, W_e_scales, W_o_words, W_o_scales
         x_tiles = {}
         grouped_tiles = {}
         mx_tiles = {}
+        out_tiles = {}
 
-        def load(g):
-            n0, parity, c0 = CHUNKS[g]
-            x_sb = x_pool.tile([P, BLOCKS, F_IN], BF16, name="x_sb", tag="x_sb")
-            nc.sync.dma_start(out=x_sb[:], in_=x[n0 : n0 + P, parity, c0 : c0 + BLOCKS, :])
-            x_tiles[g] = x_sb
+        def load(s):
+            n0, parity = CHUNKS[s]
+            x_sb = x_pool.tile([P, COMPONENTS, F_IN], BF16, name="x_sb", tag="x_sb")
+            nc.sync.dma_start(out=x_sb[:], in_=x[n0 : n0 + P, parity])
+            x_tiles[s] = x_sb
 
         def transpose(g):
-            x_words = x_tiles[g][:].bitcast(F32)
+            s, c0 = g // CHUNK_ROUNDS, g % CHUNK_ROUNDS * BLOCKS
+            x_words = x_tiles[s][:].bitcast(F32)
             grouped = grouped_pool.tile(
                 [P, BLOCKS * P * PACK], BF16, align_bytes=64, name="grouped", tag="grouped"
             )
@@ -96,9 +95,10 @@ def tile_dense_pa_t_e_kernel(tc, x, W_e_words, W_e_scales, W_o_words, W_o_scales
                 for j in range(BANK_BLOCKS):
                     for u in range(2):
                         nc.tensor.transpose(
-                            xt[:, j, u, :], x_words[:, first + j, u:WORDS:2], ident[:]
+                            xt[:, j, u, :], x_words[:, c0 + first + j, u:WORDS:2], ident[:]
                         )
-                nc.vector.tensor_copy(
+                copy = nc.scalar.copy if bank == BANKS - 1 else nc.vector.tensor_copy
+                copy(
                     out=grouped_words[:, first : first + BANK_BLOCKS],
                     in_=xt[:].rearrange("p j u r -> p j r u"),
                 )
@@ -117,10 +117,14 @@ def tile_dense_pa_t_e_kernel(tc, x, W_e_words, W_e_scales, W_o_words, W_o_scales
                 )
             mx_tiles[g] = (codes, planes)
 
-        def multiply_and_store(g):
-            n0, parity, c0 = CHUNKS[g]
+        def multiply(g):
+            s, c0 = g // CHUNK_ROUNDS, g % CHUNK_ROUNDS * BLOCKS
+            parity = CHUNKS[s][1]
             codes, planes = mx_tiles[g]
-            out_sb = out_pool.tile([P, BLOCKS * F_OUT], F32, name="out_sb", tag="out_sb")
+            if c0 == 0:
+                out_tiles[s] = out_pool.tile(
+                    [P, COMPONENTS * F_OUT], F32, name="out_sb", tag="out_sb"
+                )
             for bank in range(BANKS):
                 first = bank * BANK_BLOCKS
                 acc = psum_o.tile([P, BANK_BLOCKS * F_OUT], F32, name="acc", tag="acc")
@@ -136,29 +140,35 @@ def tile_dense_pa_t_e_kernel(tc, x, W_e_words, W_e_scales, W_o_words, W_o_scales
                         start=True,
                         stop=True,
                     )
-                result = out_sb[:, first * F_OUT : (first + BANK_BLOCKS) * F_OUT]
-                if parity == 0 and c0 + first == 0:
+                c = c0 + first
+                result = out_tiles[s][:, c * F_OUT : (c + BANK_BLOCKS) * F_OUT]
+                if parity == 0 and c == 0:
                     nc.vector.tensor_tensor(
                         out=result, in0=acc[:], in1=bias_pair[:], op=mybir.AluOpType.add
                     )
                 else:
                     nc.scalar.copy(out=result, in_=acc[:])
+
+        def store(s):
+            n0, parity = CHUNKS[s]
             nc.sync.dma_start(
-                out=out[n0 : n0 + P, parity, c0 : c0 + BLOCKS, :].rearrange("n c f -> n (c f)"),
-                in_=out_sb[:],
+                out=out[n0 : n0 + P, parity].rearrange("n c f -> n (c f)"), in_=out_tiles[s][:]
             )
 
-        for g in range(LOADS_AHEAD):
-            load(g)
-            if g == 0:
+        for s in range(LOADS_AHEAD):
+            load(s)
+            if s == 0:
                 load_weights(0, W_e_words, W_e_scales)
-            if g == 1:
+            if s == 1:
                 load_weights(1, W_o_words, W_o_scales)
         transpose(0)
-        for g in range(len(CHUNKS)):
-            if g + LOADS_AHEAD < len(CHUNKS):
-                load(g + LOADS_AHEAD)
+        for g in range(ROUNDS):
             quantise(g)
-            if g + 1 < len(CHUNKS):
+            if g + 1 < ROUNDS:
                 transpose(g + 1)
-            multiply_and_store(g)
+            multiply(g)
+            if (g + 1) % CHUNK_ROUNDS == 0:
+                s = g // CHUNK_ROUNDS
+                if s + LOADS_AHEAD < len(CHUNKS):
+                    load(s + LOADS_AHEAD)
+                store(s)

@@ -23,8 +23,6 @@ BANK_BLOCKS = 2
 BANKS = BLOCKS // BANK_BLOCKS
 CHUNK_ROUNDS = COMPONENTS // BLOCKS
 ROUNDS = len(CHUNKS) * CHUNK_ROUNDS
-LOADS_AHEAD = 4
-OUT_BUFS = 4
 
 FLOPS = 2 * ITEMS * PARITIES * COMPONENTS * F_IN * F_OUT
 
@@ -34,10 +32,9 @@ def tile_dense_pa_t_e_kernel(tc, x, W_e_words, W_e_scales, W_o_words, W_o_scales
     with ExitStack() as ctx:
         ctx.enter_context(tc.manual_schedule())
         consts = ctx.enter_context(tc.tile_pool(name="consts", bufs=1))
-        x_pool = ctx.enter_context(tc.tile_pool(name="x_pool", bufs=LOADS_AHEAD))
+        x_pool = ctx.enter_context(tc.tile_pool(name="x_pool", bufs=len(CHUNKS)))
         grouped_pool = ctx.enter_context(tc.tile_pool(name="grouped_pool", bufs=2))
         mx_pool = ctx.enter_context(tc.tile_pool(name="mx_pool", bufs=3))
-        out_pool = ctx.enter_context(tc.tile_pool(name="out_pool", bufs=OUT_BUFS))
         psum_t = ctx.enter_context(tc.psum_pool(name="psum_t", bufs=BANKS))
         psum_o = ctx.enter_context(tc.psum_pool(name="psum_o", bufs=BANKS))
 
@@ -122,9 +119,7 @@ def tile_dense_pa_t_e_kernel(tc, x, W_e_words, W_e_scales, W_o_words, W_o_scales
             parity = CHUNKS[s][1]
             codes, planes = mx_tiles[g]
             if c0 == 0:
-                out_tiles[s] = out_pool.tile(
-                    [P, COMPONENTS * F_OUT], F32, name="out_sb", tag="out_sb"
-                )
+                out_tiles[s] = x_tiles[s][:].rearrange("p c f -> p (c f)").bitcast(F32)
             for bank in range(BANKS):
                 first = bank * BANK_BLOCKS
                 acc = psum_o.tile([P, BANK_BLOCKS * F_OUT], F32, name="acc", tag="acc")
@@ -152,10 +147,10 @@ def tile_dense_pa_t_e_kernel(tc, x, W_e_words, W_e_scales, W_o_words, W_o_scales
         def store(s):
             n0, parity = CHUNKS[s]
             nc.sync.dma_start(
-                out=out[n0 : n0 + P, parity].rearrange("n c f -> n (c f)"), in_=out_tiles[s][:]
+                out=out[n0 : n0 + P, parity].rearrange("n c f -> n (c f)"), in_=out_tiles[s]
             )
 
-        for s in range(LOADS_AHEAD):
+        for s in range(len(CHUNKS)):
             load(s)
             if s == 0:
                 load_weights(0, W_e_words, W_e_scales)
@@ -168,7 +163,4 @@ def tile_dense_pa_t_e_kernel(tc, x, W_e_words, W_e_scales, W_o_words, W_o_scales
                 transpose(g + 1)
             multiply(g)
             if (g + 1) % CHUNK_ROUNDS == 0:
-                s = g // CHUNK_ROUNDS
-                if s + LOADS_AHEAD < len(CHUNKS):
-                    load(s + LOADS_AHEAD)
-                store(s)
+                store(g // CHUNK_ROUNDS)

@@ -49,11 +49,14 @@ def tile_dense_pa_t_e_kernel(tc, x, W_e_words, W_e_scales, W_o_words, W_o_scales
         nc.vector.memset(ones[:], 1.0)
         bias_rows = consts.tile([P, BANK_BLOCKS * F_OUT], BF16)
         nc.vector.memset(bias_rows[:], 0.0)
-        nc.scalar.dma_start(out=bias_rows[0:1, 0:F_OUT], in_=b.unsqueeze(0))
-        bias_psum = psum_o.tile([P, BANK_BLOCKS * F_OUT], F32, name="acc", tag="acc")
-        nc.tensor.matmul(out=bias_psum[:], lhsT=ones[:], rhs=bias_rows[:], start=True, stop=True)
         bias_pair = consts.tile([P, BANK_BLOCKS * F_OUT], F32)
-        nc.vector.tensor_copy(out=bias_pair[:], in_=bias_psum[:])
+
+        def spread_bias():
+            bias_psum = psum_o.tile([P, BANK_BLOCKS * F_OUT], F32, name="acc", tag="acc")
+            nc.tensor.matmul(
+                out=bias_psum[:], lhsT=ones[:], rhs=bias_rows[:], start=True, stop=True
+            )
+            nc.vector.tensor_copy(out=bias_pair[:], in_=bias_psum[:])
 
         def load_weights(parity, words, scales):
             by_row = scales.rearrange("l (q r) n -> r q l n", r=4)
@@ -71,10 +74,14 @@ def tile_dense_pa_t_e_kernel(tc, x, W_e_words, W_e_scales, W_o_words, W_o_scales
         mx_tiles = {}
         out_tiles = {}
 
-        def load(s):
+        def load(s, pieces):
             n0, parity = CHUNKS[s]
             x_sb = x_pool.tile([P, COMPONENTS, F_IN], BF16, name="x_sb", tag="x_sb")
-            nc.sync.dma_start(out=x_sb[:], in_=x[n0 : n0 + P, parity])
+            step = COMPONENTS // pieces
+            for c in range(0, COMPONENTS, step):
+                nc.sync.dma_start(out=x_sb[:, c : c + step], in_=x[n0 : n0 + P, parity, c : c + step])
+                if s == 0 and c == 0:
+                    nc.sync.dma_start(out=bias_rows[0:1, 0:F_OUT], in_=b.unsqueeze(0))
             x_tiles[s] = x_sb
 
         def transpose(g):
@@ -144,23 +151,28 @@ def tile_dense_pa_t_e_kernel(tc, x, W_e_words, W_e_scales, W_o_words, W_o_scales
                 else:
                     nc.scalar.copy(out=result, in_=acc[:])
 
-        def store(s):
+        def store(s, c0, c1):
             n0, parity = CHUNKS[s]
             nc.sync.dma_start(
-                out=out[n0 : n0 + P, parity].rearrange("n c f -> n (c f)"), in_=out_tiles[s]
+                out=out[n0 : n0 + P, parity, c0:c1].rearrange("n c f -> n (c f)"),
+                in_=out_tiles[s][:, c0 * F_OUT : c1 * F_OUT],
             )
 
         for s in range(len(CHUNKS)):
-            load(s)
+            load(s, CHUNK_ROUNDS if s == 0 else 1)
             if s == 0:
                 load_weights(0, W_e_words, W_e_scales)
             if s == 1:
                 load_weights(1, W_o_words, W_o_scales)
         transpose(0)
+        spread_bias()
         for g in range(ROUNDS):
             quantise(g)
             if g + 1 < ROUNDS:
                 transpose(g + 1)
             multiply(g)
-            if (g + 1) % CHUNK_ROUNDS == 0:
-                store(g // CHUNK_ROUNDS)
+            s = g // CHUNK_ROUNDS
+            if s == len(CHUNKS) - 1:
+                store(s, g % CHUNK_ROUNDS * BLOCKS, (g % CHUNK_ROUNDS + 1) * BLOCKS)
+            elif (g + 1) % CHUNK_ROUNDS == 0:
+                store(s, 0, COMPONENTS)

@@ -32,7 +32,6 @@ def tile_dense_pa_t_e_kernel(tc, x, W_e_words, W_e_scales, W_o_words, W_o_scales
     with ExitStack() as ctx:
         ctx.enter_context(tc.manual_schedule())
         consts = ctx.enter_context(tc.tile_pool(name="consts", bufs=1))
-        x_pool = ctx.enter_context(tc.tile_pool(name="x_pool", bufs=len(CHUNKS)))
         grouped_pool = ctx.enter_context(tc.tile_pool(name="grouped_pool", bufs=2))
         mx_pool = ctx.enter_context(tc.tile_pool(name="mx_pool", bufs=3))
         psum_t = ctx.enter_context(tc.psum_pool(name="psum_t", bufs=BANKS))
@@ -69,24 +68,33 @@ def tile_dense_pa_t_e_kernel(tc, x, W_e_words, W_e_scales, W_o_words, W_o_scales
                 in_=words.rearrange("l p n t -> p l (n t)").bitcast(I32),
             )
 
-        x_tiles = {}
+        x_all = consts.tile([P, len(CHUNKS), COMPONENTS, F_IN], BF16)
+        out_all = x_all[:].rearrange("p s c f -> p s (c f)").bitcast(F32)
         grouped_tiles = {}
         mx_tiles = {}
-        out_tiles = {}
 
-        def load(s, pieces):
-            n0, parity = CHUNKS[s]
-            x_sb = x_pool.tile([P, COMPONENTS, F_IN], BF16, name="x_sb", tag="x_sb")
-            step = COMPONENTS // pieces
-            for c in range(0, COMPONENTS, step):
-                nc.sync.dma_start(out=x_sb[:, c : c + step], in_=x[n0 : n0 + P, parity, c : c + step])
-                if s == 0 and c == 0:
-                    nc.sync.dma_start(out=bias_rows[0:1, 0:F_OUT], in_=b.unsqueeze(0))
-            x_tiles[s] = x_sb
+        def in_hbm(tensor, s0, s1):
+            if s1 - s0 == 1:
+                n0, parity = CHUNKS[s0]
+                return tensor[n0 : n0 + P, parity : parity + 1].rearrange("n a c f -> n a (c f)")
+            return tensor[CHUNKS[s0][0] : CHUNKS[s1 - 1][0] + P].rearrange(
+                "(t n) a c f -> n t (a c f)", n=P
+            )
+
+        def in_sbuf(view, s0, s1):
+            if s1 - s0 == 1:
+                return view[:, s0:s1]
+            return view[:, s0:s1].rearrange("p (t a) w -> p t (a w)", a=PARITIES)
+
+        def load(s0, s1):
+            nc.sync.dma_start(
+                out=in_sbuf(x_all[:].rearrange("p s c f -> p s (c f)"), s0, s1),
+                in_=in_hbm(x, s0, s1),
+            )
 
         def transpose(g):
             s, c0 = g // CHUNK_ROUNDS, g % CHUNK_ROUNDS * BLOCKS
-            x_words = x_tiles[s][:].bitcast(F32)
+            x_words = x_all[:, s].bitcast(F32)
             grouped = grouped_pool.tile(
                 [P, BLOCKS * P * PACK], BF16, align_bytes=64, name="grouped", tag="grouped"
             )
@@ -125,8 +133,6 @@ def tile_dense_pa_t_e_kernel(tc, x, W_e_words, W_e_scales, W_o_words, W_o_scales
             s, c0 = g // CHUNK_ROUNDS, g % CHUNK_ROUNDS * BLOCKS
             parity = CHUNKS[s][1]
             codes, planes = mx_tiles[g]
-            if c0 == 0:
-                out_tiles[s] = x_tiles[s][:].rearrange("p c f -> p (c f)").bitcast(F32)
             for bank in range(BANKS):
                 first = bank * BANK_BLOCKS
                 acc = psum_o.tile([P, BANK_BLOCKS * F_OUT], F32, name="acc", tag="acc")
@@ -143,7 +149,7 @@ def tile_dense_pa_t_e_kernel(tc, x, W_e_words, W_e_scales, W_o_words, W_o_scales
                         stop=True,
                     )
                 c = c0 + first
-                result = out_tiles[s][:, c * F_OUT : (c + BANK_BLOCKS) * F_OUT]
+                result = out_all[:, s, c * F_OUT : (c + BANK_BLOCKS) * F_OUT]
                 if parity == 0 and c == 0:
                     nc.vector.tensor_tensor(
                         out=result, in0=acc[:], in1=bias_pair[:], op=mybir.AluOpType.add
@@ -151,19 +157,18 @@ def tile_dense_pa_t_e_kernel(tc, x, W_e_words, W_e_scales, W_o_words, W_o_scales
                 else:
                     nc.scalar.copy(out=result, in_=acc[:])
 
-        def store(s, c0, c1):
-            n0, parity = CHUNKS[s]
-            nc.sync.dma_start(
-                out=out[n0 : n0 + P, parity, c0:c1].rearrange("n c f -> n (c f)"),
-                in_=out_tiles[s][:, c0 * F_OUT : c1 * F_OUT],
-            )
+        def store(s0, s1):
+            nc.sync.dma_start(out=in_hbm(out, s0, s1), in_=in_sbuf(out_all, s0, s1))
 
-        for s in range(len(CHUNKS)):
-            load(s, CHUNK_ROUNDS if s == 0 else 1)
-            if s == 0:
-                load_weights(0, W_e_words, W_e_scales)
-            if s == 1:
-                load_weights(1, W_o_words, W_o_scales)
+        load(0, 1)
+        nc.sync.dma_start(out=bias_rows[0:1, 0:F_OUT], in_=b.unsqueeze(0))
+        load_weights(0, W_e_words, W_e_scales)
+        load(1, 2)
+        load_weights(1, W_o_words, W_o_scales)
+        load(2, 4)
+        load(4, 6)
+        load(6, 8)
+        stores_after = {3: (0, 4), 5: (4, 6), 6: (6, 7), 7: (7, 8)}
         transpose(0)
         spread_bias()
         for g in range(ROUNDS):
@@ -171,8 +176,5 @@ def tile_dense_pa_t_e_kernel(tc, x, W_e_words, W_e_scales, W_o_words, W_o_scales
             if g + 1 < ROUNDS:
                 transpose(g + 1)
             multiply(g)
-            s = g // CHUNK_ROUNDS
-            if s == len(CHUNKS) - 1:
-                store(s, g % CHUNK_ROUNDS * BLOCKS, (g % CHUNK_ROUNDS + 1) * BLOCKS)
-            elif (g + 1) % CHUNK_ROUNDS == 0:
-                store(s, 0, COMPONENTS)
+            if (g + 1) % CHUNK_ROUNDS == 0 and g // CHUNK_ROUNDS in stores_after:
+                store(*stores_after[g // CHUNK_ROUNDS])

@@ -92,6 +92,13 @@ def tile_dense_pa_t_e_kernel(tc, x, W_e_words, W_e_scales, W_o_words, W_o_scales
                 in_=in_hbm(x, s0, s1),
             )
 
+        def load_round(g):
+            s, c0 = g // CHUNK_ROUNDS, g % CHUNK_ROUNDS * BLOCKS
+            n0, parity = CHUNKS[s]
+            nc.sync.dma_start(
+                out=x_all[:, s, c0 : c0 + BLOCKS], in_=x[n0 : n0 + P, parity, c0 : c0 + BLOCKS]
+            )
+
         def transpose(g):
             s, c0 = g // CHUNK_ROUNDS, g % CHUNK_ROUNDS * BLOCKS
             x_words = x_all[:, s].bitcast(F32)
@@ -160,15 +167,25 @@ def tile_dense_pa_t_e_kernel(tc, x, W_e_words, W_e_scales, W_o_words, W_o_scales
         def store(s0, s1):
             nc.sync.dma_start(out=in_hbm(out, s0, s1), in_=in_sbuf(out_all, s0, s1))
 
-        load(0, 1)
+        def store_round(g):
+            s, c0 = g // CHUNK_ROUNDS, g % CHUNK_ROUNDS * BLOCKS
+            n0, parity = CHUNKS[s]
+            nc.sync.dma_start(
+                out=out[n0 : n0 + P, parity, c0 : c0 + BLOCKS].rearrange("n c f -> n (c f)"),
+                in_=out_all[:, s, c0 * F_OUT : (c0 + BLOCKS) * F_OUT],
+            )
+
+        load_round(0)
         nc.sync.dma_start(out=bias_rows[0:1, 0:F_OUT], in_=b.unsqueeze(0))
+        load_round(1)
         load_weights(0, W_e_words, W_e_scales)
         load(1, 2)
         load_weights(1, W_o_words, W_o_scales)
-        load(2, 4)
+        load(2, 3)
+        load(3, 4)
         load(4, 6)
         load(6, 8)
-        stores_after = {3: (0, 4), 5: (4, 6), 6: (6, 7), 7: (7, 8)}
+        stores_after = {1: (0, 2), 3: (2, 4), 5: (4, 6), 6: (6, 7)}
         transpose(0)
         spread_bias()
         for g in range(ROUNDS):
@@ -176,5 +193,7 @@ def tile_dense_pa_t_e_kernel(tc, x, W_e_words, W_e_scales, W_o_words, W_o_scales
             if g + 1 < ROUNDS:
                 transpose(g + 1)
             multiply(g)
-            if (g + 1) % CHUNK_ROUNDS == 0 and g // CHUNK_ROUNDS in stores_after:
+            if g // CHUNK_ROUNDS == len(CHUNKS) - 1:
+                store_round(g)
+            elif (g + 1) % CHUNK_ROUNDS == 0 and g // CHUNK_ROUNDS in stores_after:
                 store(*stores_after[g // CHUNK_ROUNDS])

@@ -68,7 +68,7 @@ def tile_dense_pa_t_e_kernel(tc, x, W_e_words, W_e_scales, W_o_words, W_o_scales
                 in_=words.rearrange("l p n t -> p l (n t)").bitcast(I32),
             )
 
-        x_all = consts.tile([P, len(CHUNKS), COMPONENTS, F_IN], BF16)
+        x_all = consts.tile([P, len(CHUNKS), COMPONENTS, F_IN], BF16, align_bytes=4096)
         out_all = x_all[:].rearrange("p s c f -> p s (c f)").bitcast(F32)
         grouped_tiles = {}
         mx_tiles = {}

@@ -37,16 +37,16 @@ def tile_dense_pa_t_e_kernel(tc, x, W_e_words, W_e_scales, W_o_words, W_o_scales
         psum_t = ctx.enter_context(tc.psum_pool(name="psum_t", bufs=BANKS))
         psum_o = ctx.enter_context(tc.psum_pool(name="psum_o", bufs=BANKS))
 
-        w_scales = consts.tile([P, PARITIES, DEGREES, F_OUT], U8, align_bytes=64)
+        w_scales = consts.tile([P, PARITIES, DEGREES, F_OUT], U8, align_bytes=4096)
         nc.vector.memset(w_scales[:].rearrange("p a l n -> p (a l n)").bitcast(I32), 0)
-        w_words = consts.tile([P, PARITIES, DEGREES, F_OUT], U32, align_bytes=64)
+        w_words = consts.tile([P, PARITIES, DEGREES, F_OUT], U32, align_bytes=4096)
 
         ident = consts.tile([P, P], F32)
         make_identity(nc, ident[:])
 
         ones = consts.tile([P, P], BF16)
         nc.vector.memset(ones[:], 1.0)
-        bias_rows = consts.tile([P, BANK_BLOCKS * F_OUT], BF16)
+        bias_rows = consts.tile([P, BANK_BLOCKS * F_OUT], BF16, align_bytes=256)
         nc.vector.memset(bias_rows[:], 0.0)
         bias_pair = consts.tile([P, BANK_BLOCKS * F_OUT], F32)
 

@@ -37,8 +37,8 @@ def tile_dense_pa_t_e_kernel(tc, x, W_e_words, W_e_scales, W_o_words, W_o_scales
         psum_t = ctx.enter_context(tc.psum_pool(name="psum_t", bufs=BANKS))
         psum_o = ctx.enter_context(tc.psum_pool(name="psum_o", bufs=BANKS))
 
-        w_scales = consts.tile([P, PARITIES, DEGREES, F_OUT], U8, align_bytes=4096)
-        nc.vector.memset(w_scales[:].rearrange("p a l n -> p (a l n)").bitcast(I32), 0)
+        w_scales = consts.tile([P, PARITIES, F_OUT], U8, align_bytes=4096)
+        nc.vector.memset(w_scales[:].rearrange("p a n -> p (a n)").bitcast(I32), 0)
         w_words = consts.tile([P, PARITIES, DEGREES, F_OUT], U32, align_bytes=4096)
 
         ident = consts.tile([P, P], F32)
@@ -58,10 +58,10 @@ def tile_dense_pa_t_e_kernel(tc, x, W_e_words, W_e_scales, W_o_words, W_o_scales
             nc.vector.tensor_copy(out=bias_pair[:], in_=bias_psum[:])
 
         def load_weights(parity, words, scales):
-            by_row = scales.rearrange("l (q r) n -> r q l n", r=4)
-            for r in range(4):
+            for q in range(4):
                 nc.sync.dma_start(
-                    out=w_scales[r : P : 32, parity].bitcast(I32), in_=by_row[r].bitcast(I32)
+                    out=w_scales[32 * q : 32 * q + 16, parity].bitcast(I32),
+                    in_=scales[:, 4 * q : 4 * q + 4].bitcast(I32),
                 )
             nc.sync.dma_start(
                 out=w_words[:, parity].bitcast(I32),
@@ -151,7 +151,7 @@ def tile_dense_pa_t_e_kernel(tc, x, W_e_words, W_e_scales, W_o_words, W_o_scales
                         lhsT=codes[:, items].bitcast(FP8X4),
                         lhsT_scale=planes[:, items],
                         rhs=w_words[:, parity, degree, :].bitcast(FP8X4),
-                        rhs_scale=w_scales[:, parity, degree, :],
+                        rhs_scale=w_scales[4 * degree : P, parity, :],
                         start=True,
                         stop=True,
                     )

from contextlib import ExitStack

import concourse.mybir as mybir
from concourse.masks import make_identity

F32 = mybir.dt.float32
BF16 = mybir.dt.bfloat16
I32 = mybir.dt.int32
U32 = mybir.dt.uint32
U8 = mybir.dt.uint8
FP8X4 = mybir.dt.float8_e4m3fn_x4

P = 128
PACK = 4
ITEMS, PARITIES, COMPONENTS, F_IN, F_OUT = 512, 2, 16, 512, 256
DEGREES = 4
DEGREE_OF = [l for l in range(DEGREES) for m in range(2 * l + 1)]
WORDS = F_IN // 2

CHUNKS = [(n0, parity) for n0 in range(0, ITEMS, P) for parity in range(PARITIES)]
BLOCKS = 8
BANK_BLOCKS = 2
BANKS = BLOCKS // BANK_BLOCKS
CHUNK_ROUNDS = COMPONENTS // BLOCKS
ROUNDS = len(CHUNKS) * CHUNK_ROUNDS

FLOPS = 2 * ITEMS * PARITIES * COMPONENTS * F_IN * F_OUT


def tile_dense_pa_t_e_kernel(tc, x, W_e_words, W_e_scales, W_o_words, W_o_scales, b, out):
    nc = tc.nc
    with ExitStack() as ctx:
        ctx.enter_context(tc.manual_schedule())
        consts = ctx.enter_context(tc.tile_pool(name="consts", bufs=1))
        grouped_pool = ctx.enter_context(tc.tile_pool(name="grouped_pool", bufs=2))
        mx_pool = ctx.enter_context(tc.tile_pool(name="mx_pool", bufs=3))
        psum_t = ctx.enter_context(tc.psum_pool(name="psum_t", bufs=BANKS))
        psum_o = ctx.enter_context(tc.psum_pool(name="psum_o", bufs=BANKS))

        w_scales = consts.tile([P, PARITIES, F_OUT], U8, align_bytes=4096)
        nc.vector.memset(w_scales[:].rearrange("p a n -> p (a n)").bitcast(I32), 0)
        w_words = consts.tile([P, PARITIES, DEGREES, F_OUT], U32, align_bytes=4096)

        ident = consts.tile([P, P], F32)
        make_identity(nc, ident[:])

        ones = consts.tile([P, P], BF16)
        nc.vector.memset(ones[:], 1.0)
        bias_rows = consts.tile([P, BANK_BLOCKS * F_OUT], BF16, align_bytes=256)
        nc.vector.memset(bias_rows[:], 0.0)
        bias_pair = consts.tile([P, BANK_BLOCKS * F_OUT], F32)

        def spread_bias():
            bias_psum = psum_o.tile([P, BANK_BLOCKS * F_OUT], F32, name="acc", tag="acc")
            nc.tensor.matmul(
                out=bias_psum[:], lhsT=ones[:], rhs=bias_rows[:], start=True, stop=True
            )
            nc.vector.tensor_copy(out=bias_pair[:], in_=bias_psum[:])

        def load_weights(parity, words, scales):
            for q in range(4):
                nc.sync.dma_start(
                    out=w_scales[32 * q : 32 * q + 16, parity].bitcast(I32),
                    in_=scales[:, 4 * q : 4 * q + 4].bitcast(I32),
                )
            nc.sync.dma_start(
                out=w_words[:, parity].bitcast(I32),
                in_=words.rearrange("l p n t -> p l (n t)").bitcast(I32),
            )

        x_all = consts.tile([P, len(CHUNKS), COMPONENTS, F_IN], BF16, align_bytes=4096)
        out_all = x_all[:].rearrange("p s c f -> p s (c f)").bitcast(F32)
        grouped_tiles = {}
        mx_tiles = {}

        def in_hbm(tensor, s0, s1):
            if s1 - s0 == 1:
                n0, parity = CHUNKS[s0]
                return tensor[n0 : n0 + P, parity : parity + 1].rearrange("n a c f -> n a (c f)")
            return tensor[CHUNKS[s0][0] : CHUNKS[s1 - 1][0] + P].rearrange(
                "(t n) a c f -> n t (a c f)", n=P
            )

        def in_sbuf(view, s0, s1):
            if s1 - s0 == 1:
                return view[:, s0:s1]
            return view[:, s0:s1].rearrange("p (t a) w -> p t (a w)", a=PARITIES)

        def load(s0, s1):
            nc.sync.dma_start(
                out=in_sbuf(x_all[:].rearrange("p s c f -> p s (c f)"), s0, s1),
                in_=in_hbm(x, s0, s1),
            )

        def load_round(g):
            s, c0 = g // CHUNK_ROUNDS, g % CHUNK_ROUNDS * BLOCKS
            n0, parity = CHUNKS[s]
            nc.sync.dma_start(
                out=x_all[:, s, c0 : c0 + BLOCKS], in_=x[n0 : n0 + P, parity, c0 : c0 + BLOCKS]
            )

        def transpose(g):
            s, c0 = g // CHUNK_ROUNDS, g % CHUNK_ROUNDS * BLOCKS
            x_words = x_all[:, s].bitcast(F32)
            grouped = grouped_pool.tile(
                [P, BLOCKS * P * PACK], BF16, align_bytes=64, name="grouped", tag="grouped"
            )
            grouped_words = grouped[:].bitcast(F32).rearrange(
                "p (i r u) -> p i r u", i=BLOCKS, u=2
            )
            for bank in range(BANKS):
                first = bank * BANK_BLOCKS
                xt = psum_t.tile([P, BANK_BLOCKS, 2, P], F32, name="xt", tag="xt")
                for j in range(BANK_BLOCKS):
                    for u in range(2):
                        nc.tensor.transpose(
                            xt[:, j, u, :], x_words[:, c0 + first + j, u:WORDS:2], ident[:]
                        )
                copy = nc.scalar.copy if bank == BANKS - 1 else nc.vector.tensor_copy
                copy(
                    out=grouped_words[:, first : first + BANK_BLOCKS],
                    in_=xt[:].rearrange("p j u r -> p j r u"),
                )
            grouped_tiles[g] = grouped

        def quantise(g):
            codes = mx_pool.tile([P, BLOCKS * P], U32, align_bytes=64, name="codes", tag="codes")
            planes = mx_pool.tile([P, BLOCKS * P], U8, align_bytes=64, name="planes", tag="planes")
            half = BLOCKS * P // 2
            for h in range(2):
                cols = slice(h * half, (h + 1) * half)
                nc.vector.quantize_mx(
                    out=codes[:, cols].bitcast(FP8X4),
                    scales=planes[:, cols],
                    in_=grouped_tiles[g][:, h * half * PACK : (h + 1) * half * PACK],
                )
            mx_tiles[g] = (codes, planes)

        def multiply(g):
            s, c0 = g // CHUNK_ROUNDS, g % CHUNK_ROUNDS * BLOCKS
            parity = CHUNKS[s][1]
            codes, planes = mx_tiles[g]
            for bank in range(BANKS):
                first = bank * BANK_BLOCKS
                acc = psum_o.tile([P, BANK_BLOCKS * F_OUT], F32, name="acc", tag="acc")
                for j in range(BANK_BLOCKS):
                    items = slice((first + j) * P, (first + j + 1) * P)
                    degree = DEGREE_OF[c0 + first + j]
                    nc.tensor.matmul_mx(
                        out=acc[:, j * F_OUT : (j + 1) * F_OUT],
                        lhsT=codes[:, items].bitcast(FP8X4),
                        lhsT_scale=planes[:, items],
                        rhs=w_words[:, parity, degree, :].bitcast(FP8X4),
                        rhs_scale=w_scales[4 * degree : P, parity, :],
                        start=True,
                        stop=True,
                    )
                c = c0 + first
                result = out_all[:, s, c * F_OUT : (c + BANK_BLOCKS) * F_OUT]
                if parity == 0 and c == 0:
                    nc.vector.tensor_tensor(
                        out=result, in0=acc[:], in1=bias_pair[:], op=mybir.AluOpType.add
                    )
                else:
                    nc.scalar.copy(out=result, in_=acc[:])

        def store(s0, s1):
            nc.sync.dma_start(out=in_hbm(out, s0, s1), in_=in_sbuf(out_all, s0, s1))

        def store_round(g):
            s, c0 = g // CHUNK_ROUNDS, g % CHUNK_ROUNDS * BLOCKS
            n0, parity = CHUNKS[s]
            nc.sync.dma_start(
                out=out[n0 : n0 + P, parity, c0 : c0 + BLOCKS].rearrange("n c f -> n (c f)"),
                in_=out_all[:, s, c0 * F_OUT : (c0 + BLOCKS) * F_OUT],
            )

        load_round(0)
        nc.sync.dma_start(out=bias_rows[0:1, 0:F_OUT], in_=b.unsqueeze(0))
        load_round(1)
        load_weights(0, W_e_words, W_e_scales)
        load(1, 2)
        load_weights(1, W_o_words, W_o_scales)
        load(2, 3)
        load(3, 4)
        load(4, 6)
        load(6, 8)
        stores_after = {1: (0, 2), 3: (2, 4), 5: (4, 6), 6: (6, 7)}
        transpose(0)
        spread_bias()
        for g in range(ROUNDS):
            quantise(g)
            if g + 1 < ROUNDS:
                transpose(g + 1)
            multiply(g)
            if g // CHUNK_ROUNDS == len(CHUNKS) - 1:
                store_round(g)
            elif (g + 1) % CHUNK_ROUNDS == 0 and g // CHUNK_ROUNDS in stores_after:
                store(*stores_after[g // CHUNK_ROUNDS])
